import numpy as np
import ml_dtypes


def mxq(x, axis, fmt="e4m3"):
    dtype, down = {"e4m3": (ml_dtypes.float8_e4m3fn, 7), "e5m2": (ml_dtypes.float8_e5m2, 14)}[fmt]
    v = np.moveaxis(np.asarray(x, np.float32).astype(ml_dtypes.bfloat16).astype(np.float64), axis, -1)
    blocks = v.reshape(v.shape[:-1] + (-1, 32))
    amax = np.abs(blocks).max(-1, keepdims=True)
    byte = np.maximum(np.where(amax > 0, np.frexp(amax)[1] - 1 + 127, 0) - down, 1)
    scale = np.exp2(byte - 127.0)
    codes = (blocks / scale).astype(np.float32).astype(dtype).astype(np.float64)
    return np.moveaxis((codes * scale).reshape(v.shape), -1, axis)


WIDE = False


def mx_kscale(k):
    if not WIDE:
        return np.ones(k)
    levels = np.array([10, -10, 5, -5, 0])
    a = np.random.permutation(np.resize(levels, k // 512 * 4)).reshape(k // 512, 4)
    idx = np.arange(k)
    return np.exp2(a[idx // 512, idx % 128 // 32])


BF16 = ml_dtypes.bfloat16


def bf(x):
    return np.asarray(x, np.float32).astype(BF16)


def f64(x):
    return np.asarray(x).astype(np.float64)


B, S, D, H, HD, FF = 4, 2048, 512, 1, 128, 8192
EPS = 1e-05


def layer_norm(x, scale, bias):
    mu = x.mean(-1, keepdims=True)
    var = x.var(-1, keepdims=True)
    return (x - mu) / np.sqrt(var + EPS) * scale + bias


def setup_inputs():
    s = mx_kscale(D)
    return {
        "x": bf(np.random.standard_normal((B, S, D)) + 0.5 * np.random.standard_normal((B, S, 1))),
        "ln1_s": bf((1.0 + 0.1 * np.random.standard_normal(D)) * s),
        "ln1_b": bf(0.1 * np.random.standard_normal(D) * s),
        "wq_k": bf(np.random.standard_normal((D, H, HD)) / np.sqrt(D) / s[:, None, None]),
        "wq_b": bf(0.1 * np.random.standard_normal((H, HD))),
        "wk_k": bf(np.random.standard_normal((D, HD)) / np.sqrt(D) / s[:, None]),
        "wk_b": bf(0.1 * np.random.standard_normal(HD)),
        "wv_k": bf(np.random.standard_normal((D, HD)) / np.sqrt(D) / s[:, None]),
        "wv_b": bf(0.1 * np.random.standard_normal(HD)),
    }


def reference(x, ln1_s, ln1_b, wq_k, wq_b, wk_k, wk_b, wv_k, wv_b):
    h = layer_norm(f64(x), f64(ln1_s), f64(ln1_b))
    hq = mxq(h, 2, "e4m3")
    q = (hq @ mxq(f64(wq_k).reshape(D, H * HD), 0, "e4m3")).reshape(B, S, H, HD) + f64(wq_b)
    k = (hq @ mxq(f64(wk_k), 0, "e4m3")) + f64(wk_b)
    v = (hq @ mxq(f64(wv_k), 0, "e4m3")) + f64(wv_b)
    return q, k, v

@@ -1,0 +1,228 @@
+from contextlib import ExitStack
+
+import concourse.mybir as mybir
+from concourse.masks import make_identity
+
+F32 = mybir.dt.float32
+BF16 = mybir.dt.bfloat16
+U32 = mybir.dt.uint32
+U8 = mybir.dt.uint8
+FP8X4 = mybir.dt.float8_e4m3fn_x4
+ALU = mybir.AluOpType
+ACT = mybir.ActivationFunctionType
+
+P = 128
+D = 512
+PACK = 4
+E = 128
+NPROJ = 3
+TOKENS = 4 * 2048
+GT = 4
+GTOK = GT * P
+NG = TOKENS // GTOK
+EPS = 1e-05
+TRB = 5
+
+FLOPS = 2 * TOKENS * D * NPROJ * E
+
+
+def tile_transformerlayer_pa_t_kernel(
+    tc, x, ln1_s, ln1_b, wq_k, wq_b, wk_k, wk_b, wv_k, wv_b, out_0, out_1, out_2
+):
+    nc = tc.nc
+    xg = x.rearrange("b s d -> (b s) d").rearrange("(g p j) d -> g p (j d)", p=P, j=GT)
+    outs = [
+        out_0.rearrange("b s h e -> (b s h) e").rearrange("(g p j) e -> g p (j e)", p=P, j=GT),
+        out_1.rearrange("b s e -> (b s) e").rearrange("(g p j) e -> g p (j e)", p=P, j=GT),
+        out_2.rearrange("b s e -> (b s) e").rearrange("(g p j) e -> g p (j e)", p=P, j=GT),
+    ]
+
+    with ExitStack() as ctx:
+        const = ctx.enter_context(tc.tile_pool(name="const", bufs=1))
+        xpool = ctx.enter_context(tc.tile_pool(name="xpool", bufs=NG))
+        small = ctx.enter_context(tc.tile_pool(name="small", bufs=4))
+        zpool = ctx.enter_context(tc.tile_pool(name="zpool", bufs=3))
+        hpool = ctx.enter_context(tc.tile_pool(name="hpool", bufs=3))
+        qpool = ctx.enter_context(tc.tile_pool(name="qpool", bufs=3))
+        opool = ctx.enter_context(tc.tile_pool(name="opool", bufs=4))
+        psum = ctx.enter_context(tc.psum_pool(name="psum", bufs=1))
+        ctx.enter_context(tc.manual_schedule())
+
+        xt = []
+        for g in range(NG):
+            x_t = xpool.tile([P, GT, D], BF16, name="x_t")
+            nc.sync.dma_start(out=x_t[:].rearrange("p j d -> p (j d)"), in_=xg[g])
+            xt.append(x_t)
+
+        sbrow = const.tile([P, P], BF16, name="sbrow")
+        nc.vector.memset(sbrow[:], 0.0)
+        eps_t = const.tile([P, 1], F32, name="eps_t")
+        nc.vector.memset(eps_t[:], EPS)
+        nc.scalar.dma_start(out=sbrow[0:PACK, :], in_=ln1_s.rearrange("(t p) -> t p", p=P))
+        nc.scalar.dma_start(out=sbrow[PACK : 2 * PACK, :], in_=ln1_b.rearrange("(t p) -> t p", p=P))
+        wraw = const.tile([P, PACK, NPROJ * E], BF16, name="wraw")
+        nc.scalar.dma_start(out=wraw[:, :, 0:E], in_=wq_k.rearrange("(t p) h e -> p t (h e)", p=P))
+        nc.scalar.dma_start(out=wraw[:, :, E : 2 * E], in_=wk_k.rearrange("(t p) e -> p t e", p=P))
+        nc.scalar.dma_start(out=wraw[:, :, 2 * E : 3 * E], in_=wv_k.rearrange("(t p) e -> p t e", p=P))
+
+        ident = const.tile([P, P], F32, name="ident")
+        make_identity(nc, ident[:])
+        bias = const.tile([P, NPROJ, E], BF16, name="bias")
+        nc.gpsimd.dma_start(out=bias[:, 0, :], in_=wq_b.rearrange("h e -> (h e)").partition_broadcast(P))
+        nc.gpsimd.dma_start(out=bias[:, 1, :], in_=wk_b.partition_broadcast(P))
+        nc.gpsimd.dma_start(out=bias[:, 2, :], in_=wv_b.partition_broadcast(P))
+
+        sbcol = const.tile([P, 2 * PACK], F32, name="sbcol")
+        wcodes = const.tile([P, NPROJ * E], U32, name="wcodes", align_bytes=64)
+        wscl = const.tile([P, NPROJ * E], U8, name="wscl", align_bytes=64)
+
+        def setup_a():
+            sbrow32 = const.tile([P, P], F32, name="sbrow32")
+            nc.vector.tensor_copy(out=sbrow32[:], in_=sbrow[:])
+            ps = psum.tile([P, D], F32, name="ps_setup", tag="mm0")
+            nc.tensor.transpose(ps[:, 0:P], sbrow32[:], ident[:])
+            return ps
+
+        def setup_b(ps):
+            nc.vector.tensor_copy(out=sbcol[:], in_=ps[:, 0 : 2 * PACK])
+            wgrp = const.tile([P, NPROJ * E, PACK], BF16, name="wgrp", align_bytes=64)
+            nc.vector.tensor_copy(out=wgrp[:], in_=wraw[:].rearrange("p t n -> p n t"))
+            for pr in range(NPROJ):
+                cols = slice(pr * E, (pr + 1) * E)
+                nc.vector.quantize_mx(
+                    out=wcodes[:, cols].bitcast(FP8X4),
+                    scales=wscl[:, cols],
+                    in_=wgrp[:, cols, :].rearrange("p n t -> p (n t)"),
+                )
+
+        S = {}
+
+        def stats(g):
+            st = small.tile([P, GT, 6], F32, name="st")
+            mv = small.tile([P, GT, 2], F32, name="mv")
+            for j in range(GT):
+                nc.vector.bn_stats(out=st[:, j, :], in_=xt[g][:, j, :])
+            for j in range(GT):
+                nc.vector.bn_aggr(out=mv[:, j, :], in_=st[:, j, :])
+            S[("mv", g)] = mv
+
+        def rstd_of(g):
+            mv = S[("mv", g)]
+            sd = small.tile([P, GT], F32, name="sd")
+            nc.scalar.activation(out=sd[:], in_=mv[:, :, 1], func=ACT.Sqrt, bias=eps_t[:, 0:1], scale=1.0)
+            rstd = small.tile([P, GT], F32, name="rstd")
+            nc.vector.reciprocal(out=rstd[:], in_=sd[:])
+            negmu = small.tile([P, GT], F32, name="negmu")
+            nc.vector.tensor_scalar_mul(out=negmu[:], in0=mv[:, :, 0], scalar1=-1.0)
+            S[("rs", g)] = (rstd, negmu)
+
+        def normalise(g):
+            rstd, negmu = S[("rs", g)]
+            z = zpool.tile([P, GT, D], F32, name="z")
+            for j in range(GT):
+                nc.gpsimd.tensor_scalar(
+                    out=z[:, j, :],
+                    in0=xt[g][:, j, :],
+                    scalar1=negmu[:, j : j + 1],
+                    scalar2=rstd[:, j : j + 1],
+                    op0=ALU.add,
+                    op1=ALU.mult,
+                )
+            S[("z", g)] = z
+
+        def transposes(g):
+            z = S[("z", g)]
+            banks = []
+            for t in range(PACK):
+                bank = psum.tile([P, GTOK], F32, name="trb", tag="tr%d" % ((PACK * g + t) % TRB))
+                for j in range(GT):
+                    nc.tensor.transpose(bank[:, j * P : (j + 1) * P], z[:, j, t * P : (t + 1) * P], ident[:])
+                banks.append(bank)
+            S[("tr", g)] = banks
+
+        def affine(g):
+            banks = S[("tr", g)]
+            hT = hpool.tile([P, PACK, GTOK], BF16, name="hT")
+            for t in range(PACK):
+                nc.scalar.activation(
+                    out=hT[:, t, :],
+                    in_=banks[t][:],
+                    func=ACT.Identity,
+                    scale=sbcol[:, t : t + 1],
+                    bias=sbcol[:, PACK + t : PACK + t + 1],
+                )
+            S[("hT", g)] = hT
+
+        def regroup(g):
+            hT = S[("hT", g)]
+            hG = hpool.tile([P, GTOK, PACK], BF16, name="hG", align_bytes=64)
+            nc.scalar.copy(
+                out=hG[:].rearrange("p (c i) t -> p c t i", i=4),
+                in_=hT[:].rearrange("p t (c i) -> p c t i", i=4),
+            )
+            S[("hG", g)] = hG
+
+        def quantise(g):
+            hG = S[("hG", g)]
+            codes = qpool.tile([P, GTOK], U32, name="codes", align_bytes=64)
+            scl = qpool.tile([P, GTOK], U8, name="scl", align_bytes=64)
+            nc.vector.quantize_mx(
+                out=codes[:].bitcast(FP8X4), scales=scl[:], in_=hG[:].rearrange("p c t -> p (c t)")
+            )
+            S[("q", g)] = (codes, scl)
+
+        def project(g):
+            codes, scl = S[("q", g)]
+            banks = []
+            for pr in range(NPROJ):
+                bank = psum.tile([P, GT * E], F32, name="mmb", tag="mm%d" % pr)
+                wc = slice(pr * E, (pr + 1) * E)
+                for j in range(GT):
+                    tk = slice(j * P, (j + 1) * P)
+                    nc.tensor.matmul_mx(
+                        out=bank[:, j * E : (j + 1) * E],
+                        lhsT=codes[:, tk].bitcast(FP8X4),
+                        lhsT_scale=scl[:, tk],
+                        rhs=wcodes[:, wc].bitcast(FP8X4),
+                        rhs_scale=wscl[:, wc],
+                        start=True,
+                        stop=True,
+                    )
+                banks.append(bank)
+            S[("mm", g)] = banks
+
+        def finish(g):
+            banks = S[("mm", g)]
+            o = opool.tile([P, NPROJ, GT * E], F32, name="o")
+            for pr in range(NPROJ):
+                nc.vector.tensor_tensor(
+                    out=o[:, pr, :].rearrange("p (j e) -> p j e", e=E),
+                    in0=banks[pr][:].rearrange("p (j e) -> p j e", e=E),
+                    in1=bias[:, pr, :].unsqueeze(1).to_broadcast([P, GT, E]),
+                    op=ALU.add,
+                )
+                nc.sync.dma_start(out=outs[pr][g], in_=o[:, pr, :])
+
+        ps_setup = None
+        for i in range(NG + 5):
+            if 0 <= i - 1 < NG:
+                rstd_of(i - 1)
+                normalise(i - 1)
+            if 0 <= i - 2 < NG:
+                affine(i - 2)
+            if 0 <= i - 1 < NG:
+                transposes(i - 1)
+            if 0 <= i - 2 < NG:
+                regroup(i - 2)
+            if i < NG:
+                stats(i)
+            if i == 0:
+                ps_setup = setup_a()
+            if i == 1:
+                setup_b(ps_setup)
+            if 0 <= i - 3 < NG:
+                quantise(i - 3)
+            if 0 <= i - 4 < NG:
+                finish(i - 4)
+            if 0 <= i - 3 < NG:
+                project(i - 3)

@@ -22,6 +22,12 @@ GTOK = GT * P
 NG = TOKENS // GTOK
 EPS = 1e-05
 TRB = 5
+LEAD_STATS = 4
+LEAD_NORM = 2
+UNITS = 1 + NPROJ
+QUOTA_BESIDE_STATS = 3
+QUOTA_ALONE = 8
+G_COLS = 0
 
 FLOPS = 2 * TOKENS * D * NPROJ * E
 
@@ -40,9 +46,10 @@ def tile_transformerlayer_pa_t_kernel(
     with ExitStack() as ctx:
         const = ctx.enter_context(tc.tile_pool(name="const", bufs=1))
         xpool = ctx.enter_context(tc.tile_pool(name="xpool", bufs=NG))
-        small = ctx.enter_context(tc.tile_pool(name="small", bufs=4))
+        small = ctx.enter_context(tc.tile_pool(name="small", bufs=6))
         zpool = ctx.enter_context(tc.tile_pool(name="zpool", bufs=3))
-        hpool = ctx.enter_context(tc.tile_pool(name="hpool", bufs=3))
+        tpool = ctx.enter_context(tc.tile_pool(name="tpool", bufs=2))
+        hpool = ctx.enter_context(tc.tile_pool(name="hpool", bufs=6))
         qpool = ctx.enter_context(tc.tile_pool(name="qpool", bufs=3))
         opool = ctx.enter_context(tc.tile_pool(name="opool", bufs=4))
         psum = ctx.enter_context(tc.psum_pool(name="psum", bufs=1))
@@ -56,8 +63,6 @@ def tile_transformerlayer_pa_t_kernel(
 
         sbrow = const.tile([P, P], BF16, name="sbrow")
         nc.vector.memset(sbrow[:], 0.0)
-        eps_t = const.tile([P, 1], F32, name="eps_t")
-        nc.vector.memset(eps_t[:], EPS)
         nc.scalar.dma_start(out=sbrow[0:PACK, :], in_=ln1_s.rearrange("(t p) -> t p", p=P))
         nc.scalar.dma_start(out=sbrow[PACK : 2 * PACK, :], in_=ln1_b.rearrange("(t p) -> t p", p=P))
         wraw = const.tile([P, PACK, NPROJ * E], BF16, name="wraw")
@@ -75,16 +80,19 @@ def tile_transformerlayer_pa_t_kernel(
         sbcol = const.tile([P, 2 * PACK], F32, name="sbcol")
         wcodes = const.tile([P, NPROJ * E], U32, name="wcodes", align_bytes=64)
         wscl = const.tile([P, NPROJ * E], U8, name="wscl", align_bytes=64)
+        S = {}
 
-        def setup_a():
+        def gain_rows_to_psum():
             sbrow32 = const.tile([P, P], F32, name="sbrow32")
             nc.vector.tensor_copy(out=sbrow32[:], in_=sbrow[:])
             ps = psum.tile([P, D], F32, name="ps_setup", tag="mm0")
             nc.tensor.transpose(ps[:, 0:P], sbrow32[:], ident[:])
-            return ps
+            S["ps"] = ps
 
-        def setup_b(ps):
-            nc.vector.tensor_copy(out=sbcol[:], in_=ps[:, 0 : 2 * PACK])
+        def gain_columns():
+            nc.vector.tensor_copy(out=sbcol[:], in_=S["ps"][:, 0 : 2 * PACK])
+
+        def quantise_weights():
             wgrp = const.tile([P, NPROJ * E, PACK], BF16, name="wgrp", align_bytes=64)
             nc.vector.tensor_copy(out=wgrp[:], in_=wraw[:].rearrange("p t n -> p n t"))
             for pr in range(NPROJ):
@@ -95,8 +103,6 @@ def tile_transformerlayer_pa_t_kernel(
                     in_=wgrp[:, cols, :].rearrange("p n t -> p (n t)"),
                 )
 
-        S = {}
-
         def stats(g):
             st = small.tile([P, GT, 6], F32, name="st")
             mv = small.tile([P, GT, 2], F32, name="mv")
@@ -104,31 +110,30 @@ def tile_transformerlayer_pa_t_kernel(
                 nc.vector.bn_stats(out=st[:, j, :], in_=xt[g][:, j, :])
             for j in range(GT):
                 nc.vector.bn_aggr(out=mv[:, j, :], in_=st[:, j, :])
-            S[("mv", g)] = mv
+            inv = small.tile([P, GT], F32, name="inv")
+            nc.vector.tensor_scalar_add(out=inv[:], in0=mv[:, :, 1], scalar1=EPS)
+            nc.vector.reciprocal(out=inv[:], in_=inv[:])
+            S[("mv", g)] = (mv, inv)
 
-        def rstd_of(g):
-            mv = S[("mv", g)]
-            sd = small.tile([P, GT], F32, name="sd")
-            nc.scalar.activation(out=sd[:], in_=mv[:, :, 1], func=ACT.Sqrt, bias=eps_t[:, 0:1], scale=1.0)
+        def roots(g):
+            mv, inv = S[("mv", g)]
             rstd = small.tile([P, GT], F32, name="rstd")
-            nc.vector.reciprocal(out=rstd[:], in_=sd[:])
+            nc.scalar.activation(out=rstd[:], in_=inv[:], func=ACT.Sqrt)
             negmu = small.tile([P, GT], F32, name="negmu")
-            nc.vector.tensor_scalar_mul(out=negmu[:], in0=mv[:, :, 0], scalar1=-1.0)
+            nc.scalar.mul(out=negmu[:], in_=mv[:, :, 0], mul=-1.0)
             S[("rs", g)] = (rstd, negmu)
+            S[("z", g)] = zpool.tile([P, GT, D], F32, name="z")
 
-        def normalise(g):
+        def normalise(g, j):
             rstd, negmu = S[("rs", g)]
-            z = zpool.tile([P, GT, D], F32, name="z")
-            for j in range(GT):
-                nc.gpsimd.tensor_scalar(
-                    out=z[:, j, :],
-                    in0=xt[g][:, j, :],
-                    scalar1=negmu[:, j : j + 1],
-                    scalar2=rstd[:, j : j + 1],
-                    op0=ALU.add,
-                    op1=ALU.mult,
-                )
-            S[("z", g)] = z
+            nc.gpsimd.tensor_scalar(
+                out=S[("z", g)][:, j, :],
+                in0=xt[g][:, j, :],
+                scalar1=negmu[:, j : j + 1],
+                scalar2=rstd[:, j : j + 1],
+                op0=ALU.add,
+                op1=ALU.mult,
+            )
 
         def transposes(g):
             z = S[("z", g)]
@@ -142,7 +147,7 @@ def tile_transformerlayer_pa_t_kernel(
 
         def affine(g):
             banks = S[("tr", g)]
-            hT = hpool.tile([P, PACK, GTOK], BF16, name="hT")
+            hT = tpool.tile([P, PACK, GTOK], BF16, name="hT")
             for t in range(PACK):
                 nc.scalar.activation(
                     out=hT[:, t, :],
@@ -152,15 +157,21 @@ def tile_transformerlayer_pa_t_kernel(
                     bias=sbcol[:, PACK + t : PACK + t + 1],
                 )
             S[("hT", g)] = hT
+            S[("hG", g)] = hpool.tile([P, GTOK, PACK], BF16, name="hG", align_bytes=64)
 
-        def regroup(g):
-            hT = S[("hT", g)]
-            hG = hpool.tile([P, GTOK, PACK], BF16, name="hG", align_bytes=64)
-            nc.scalar.copy(
-                out=hG[:].rearrange("p (c i) t -> p c t i", i=4),
-                in_=hT[:].rearrange("p t (c i) -> p c t i", i=4),
-            )
-            S[("hG", g)] = hG
+        def regroup_views(g, lo, hi):
+            dst = S[("hG", g)][:, lo:hi, :].rearrange("p (c i) t -> p c t i", i=4)
+            src = S[("hT", g)][:, :, lo:hi].rearrange("p t (c i) -> p c t i", i=4)
+            return dst, src
+
+        def regroup_scalar(g):
+            dst, src = regroup_views(g, 0, GTOK - G_COLS)
+            nc.scalar.copy(out=dst, in_=src)
+
+        def regroup_gpsimd(g):
+            if G_COLS:
+                dst, src = regroup_views(g, GTOK - G_COLS, GTOK)
+                nc.gpsimd.tensor_scalar(out=dst, in0=src, scalar1=1.0, scalar2=0.0, op0=ALU.mult, op1=ALU.add)
 
         def quantise(g):
             hG = S[("hG", g)]
@@ -171,58 +182,73 @@ def tile_transformerlayer_pa_t_kernel(
             )
             S[("q", g)] = (codes, scl)
 
-        def project(g):
+        def project(g, pr):
             codes, scl = S[("q", g)]
-            banks = []
-            for pr in range(NPROJ):
-                bank = psum.tile([P, GT * E], F32, name="mmb", tag="mm%d" % pr)
-                wc = slice(pr * E, (pr + 1) * E)
-                for j in range(GT):
-                    tk = slice(j * P, (j + 1) * P)
-                    nc.tensor.matmul_mx(
-                        out=bank[:, j * E : (j + 1) * E],
-                        lhsT=codes[:, tk].bitcast(FP8X4),
-                        lhsT_scale=scl[:, tk],
-                        rhs=wcodes[:, wc].bitcast(FP8X4),
-                        rhs_scale=wscl[:, wc],
-                        start=True,
-                        stop=True,
-                    )
-                banks.append(bank)
-            S[("mm", g)] = banks
-
-        def finish(g):
-            banks = S[("mm", g)]
-            o = opool.tile([P, NPROJ, GT * E], F32, name="o")
-            for pr in range(NPROJ):
-                nc.vector.tensor_tensor(
-                    out=o[:, pr, :].rearrange("p (j e) -> p j e", e=E),
-                    in0=banks[pr][:].rearrange("p (j e) -> p j e", e=E),
-                    in1=bias[:, pr, :].unsqueeze(1).to_broadcast([P, GT, E]),
-                    op=ALU.add,
+            bank = psum.tile([P, GT * E], F32, name="mmb", tag="mm%d" % pr)
+            wc = slice(pr * E, (pr + 1) * E)
+            for j in range(GT):
+                tk = slice(j * P, (j + 1) * P)
+                nc.tensor.matmul_mx(
+                    out=bank[:, j * E : (j + 1) * E],
+                    lhsT=codes[:, tk].bitcast(FP8X4),
+                    lhsT_scale=scl[:, tk],
+                    rhs=wcodes[:, wc].bitcast(FP8X4),
+                    rhs_scale=wscl[:, wc],
+                    start=True,
+                    stop=True,
                 )
-                nc.sync.dma_start(out=outs[pr][g], in_=o[:, pr, :])
+            S[("mm", g, pr)] = bank
 
-        ps_setup = None
-        for i in range(NG + 5):
-            if 0 <= i - 1 < NG:
-                rstd_of(i - 1)
-                normalise(i - 1)
-            if 0 <= i - 2 < NG:
-                affine(i - 2)
-            if 0 <= i - 1 < NG:
-                transposes(i - 1)
-            if 0 <= i - 2 < NG:
-                regroup(i - 2)
-            if i < NG:
-                stats(i)
-            if i == 0:
-                ps_setup = setup_a()
-            if i == 1:
-                setup_b(ps_setup)
-            if 0 <= i - 3 < NG:
-                quantise(i - 3)
-            if 0 <= i - 4 < NG:
-                finish(i - 4)
-            if 0 <= i - 3 < NG:
-                project(i - 3)
+        def finish(g, pr):
+            if pr == 0:
+                S[("o", g)] = opool.tile([P, NPROJ, GT * E], F32, name="o")
+            o = S[("o", g)]
+            nc.vector.tensor_tensor(
+                out=o[:, pr, :].rearrange("p (j e) -> p j e", e=E),
+                in0=S[("mm", g, pr)][:].rearrange("p (j e) -> p j e", e=E),
+                in1=bias[:, pr, :].unsqueeze(1).to_broadcast([P, GT, E]),
+                op=ALU.add,
+            )
+            nc.sync.dma_start(out=outs[pr][g], in_=o[:, pr, :])
+
+        def drain(u):
+            g, k = divmod(u, UNITS)
+            if k == 0:
+                if g < NG:
+                    quantise(g)
+            else:
+                if g >= 1:
+                    finish(g - 1, k - 1)
+                if g < NG:
+                    project(g, k - 1)
+
+        drained = 0
+        for i in range(-LEAD_STATS, NG + 2):
+            if 0 <= i < NG:
+                affine(i)
+            n = i + LEAD_NORM
+            if 0 <= n < NG:
+                roots(n)
+            if 0 <= i + 1 < NG:
+                transposes(i + 1)
+            if 0 <= i < NG:
+                regroup_scalar(i)
+            for j in range(GT):
+                if 0 <= n < NG:
+                    normalise(n, j)
+                if j == GT - 2 and 0 <= i < NG:
+                    regroup_gpsimd(i)
+            quota = QUOTA_BESIDE_STATS if i + LEAD_STATS < NG else QUOTA_ALONE
+            upto = max(drained, min(UNITS * i, drained + quota))
+            for u in range(drained, upto):
+                drain(u)
+            drained = upto
+            s = i + LEAD_STATS
+            if s < NG:
+                stats(s)
+            if s == 0:
+                gain_rows_to_psum()
+            if s == 1:
+                gain_columns()
+            if s == 2:
+                quantise_weights()

@@ -27,7 +27,7 @@ LEAD_NORM = 2
 UNITS = 1 + NPROJ
 QUOTA_BESIDE_STATS = 3
 QUOTA_ALONE = 8
-G_COLS = 0
+G_COLS = 128
 
 FLOPS = 2 * TOKENS * D * NPROJ * E
 

@@ -22,12 +22,6 @@ GTOK = GT * P
 NG = TOKENS // GTOK
 EPS = 1e-05
 TRB = 5
-LEAD_STATS = 4
-LEAD_NORM = 2
-UNITS = 1 + NPROJ
-QUOTA_BESIDE_STATS = 3
-QUOTA_ALONE = 8
-G_COLS = 128
 
 FLOPS = 2 * TOKENS * D * NPROJ * E
 
@@ -46,14 +40,12 @@ def tile_transformerlayer_pa_t_kernel(
     with ExitStack() as ctx:
         const = ctx.enter_context(tc.tile_pool(name="const", bufs=1))
         xpool = ctx.enter_context(tc.tile_pool(name="xpool", bufs=NG))
-        small = ctx.enter_context(tc.tile_pool(name="small", bufs=6))
+        small = ctx.enter_context(tc.tile_pool(name="small", bufs=4))
         zpool = ctx.enter_context(tc.tile_pool(name="zpool", bufs=3))
-        tpool = ctx.enter_context(tc.tile_pool(name="tpool", bufs=2))
-        hpool = ctx.enter_context(tc.tile_pool(name="hpool", bufs=6))
+        hpool = ctx.enter_context(tc.tile_pool(name="hpool", bufs=3))
         qpool = ctx.enter_context(tc.tile_pool(name="qpool", bufs=3))
         opool = ctx.enter_context(tc.tile_pool(name="opool", bufs=4))
         psum = ctx.enter_context(tc.psum_pool(name="psum", bufs=1))
-        ctx.enter_context(tc.manual_schedule())
 
         xt = []
         for g in range(NG):
@@ -63,6 +55,8 @@ def tile_transformerlayer_pa_t_kernel(
 
         sbrow = const.tile([P, P], BF16, name="sbrow")
         nc.vector.memset(sbrow[:], 0.0)
+        eps_t = const.tile([P, 1], F32, name="eps_t")
+        nc.vector.memset(eps_t[:], EPS)
         nc.scalar.dma_start(out=sbrow[0:PACK, :], in_=ln1_s.rearrange("(t p) -> t p", p=P))
         nc.scalar.dma_start(out=sbrow[PACK : 2 * PACK, :], in_=ln1_b.rearrange("(t p) -> t p", p=P))
         wraw = const.tile([P, PACK, NPROJ * E], BF16, name="wraw")
@@ -80,19 +74,16 @@ def tile_transformerlayer_pa_t_kernel(
         sbcol = const.tile([P, 2 * PACK], F32, name="sbcol")
         wcodes = const.tile([P, NPROJ * E], U32, name="wcodes", align_bytes=64)
         wscl = const.tile([P, NPROJ * E], U8, name="wscl", align_bytes=64)
-        S = {}
 
-        def gain_rows_to_psum():
+        def setup_a():
             sbrow32 = const.tile([P, P], F32, name="sbrow32")
             nc.vector.tensor_copy(out=sbrow32[:], in_=sbrow[:])
             ps = psum.tile([P, D], F32, name="ps_setup", tag="mm0")
             nc.tensor.transpose(ps[:, 0:P], sbrow32[:], ident[:])
-            S["ps"] = ps
+            return ps
 
-        def gain_columns():
-            nc.vector.tensor_copy(out=sbcol[:], in_=S["ps"][:, 0 : 2 * PACK])
-
-        def quantise_weights():
+        def setup_b(ps):
+            nc.vector.tensor_copy(out=sbcol[:], in_=ps[:, 0 : 2 * PACK])
             wgrp = const.tile([P, NPROJ * E, PACK], BF16, name="wgrp", align_bytes=64)
             nc.vector.tensor_copy(out=wgrp[:], in_=wraw[:].rearrange("p t n -> p n t"))
             for pr in range(NPROJ):
@@ -103,6 +94,8 @@ def tile_transformerlayer_pa_t_kernel(
                     in_=wgrp[:, cols, :].rearrange("p n t -> p (n t)"),
                 )
 
+        S = {}
+
         def stats(g):
             st = small.tile([P, GT, 6], F32, name="st")
             mv = small.tile([P, GT, 2], F32, name="mv")
@@ -110,30 +103,31 @@ def tile_transformerlayer_pa_t_kernel(
                 nc.vector.bn_stats(out=st[:, j, :], in_=xt[g][:, j, :])
             for j in range(GT):
                 nc.vector.bn_aggr(out=mv[:, j, :], in_=st[:, j, :])
-            inv = small.tile([P, GT], F32, name="inv")
-            nc.vector.tensor_scalar_add(out=inv[:], in0=mv[:, :, 1], scalar1=EPS)
-            nc.vector.reciprocal(out=inv[:], in_=inv[:])
-            S[("mv", g)] = (mv, inv)
+            S[("mv", g)] = mv
 
-        def roots(g):
-            mv, inv = S[("mv", g)]
+        def rstd_of(g):
+            mv = S[("mv", g)]
+            sd = small.tile([P, GT], F32, name="sd")
+            nc.scalar.activation(out=sd[:], in_=mv[:, :, 1], func=ACT.Sqrt, bias=eps_t[:, 0:1], scale=1.0)
             rstd = small.tile([P, GT], F32, name="rstd")
-            nc.scalar.activation(out=rstd[:], in_=inv[:], func=ACT.Sqrt)
+            nc.vector.reciprocal(out=rstd[:], in_=sd[:])
             negmu = small.tile([P, GT], F32, name="negmu")
-            nc.scalar.mul(out=negmu[:], in_=mv[:, :, 0], mul=-1.0)
+            nc.vector.tensor_scalar_mul(out=negmu[:], in0=mv[:, :, 0], scalar1=-1.0)
             S[("rs", g)] = (rstd, negmu)
-            S[("z", g)] = zpool.tile([P, GT, D], F32, name="z")
 
-        def normalise(g, j):
+        def normalise(g):
             rstd, negmu = S[("rs", g)]
-            nc.gpsimd.tensor_scalar(
-                out=S[("z", g)][:, j, :],
-                in0=xt[g][:, j, :],
-                scalar1=negmu[:, j : j + 1],
-                scalar2=rstd[:, j : j + 1],
-                op0=ALU.add,
-                op1=ALU.mult,
-            )
+            z = zpool.tile([P, GT, D], F32, name="z")
+            for j in range(GT):
+                nc.gpsimd.tensor_scalar(
+                    out=z[:, j, :],
+                    in0=xt[g][:, j, :],
+                    scalar1=negmu[:, j : j + 1],
+                    scalar2=rstd[:, j : j + 1],
+                    op0=ALU.add,
+                    op1=ALU.mult,
+                )
+            S[("z", g)] = z
 
         def transposes(g):
             z = S[("z", g)]
@@ -147,7 +141,7 @@ def tile_transformerlayer_pa_t_kernel(
 
         def affine(g):
             banks = S[("tr", g)]
-            hT = tpool.tile([P, PACK, GTOK], BF16, name="hT")
+            hT = hpool.tile([P, PACK, GTOK], BF16, name="hT")
             for t in range(PACK):
                 nc.scalar.activation(
                     out=hT[:, t, :],
@@ -157,21 +151,15 @@ def tile_transformerlayer_pa_t_kernel(
                     bias=sbcol[:, PACK + t : PACK + t + 1],
                 )
             S[("hT", g)] = hT
-            S[("hG", g)] = hpool.tile([P, GTOK, PACK], BF16, name="hG", align_bytes=64)
 
-        def regroup_views(g, lo, hi):
-            dst = S[("hG", g)][:, lo:hi, :].rearrange("p (c i) t -> p c t i", i=4)
-            src = S[("hT", g)][:, :, lo:hi].rearrange("p t (c i) -> p c t i", i=4)
-            return dst, src
-
-        def regroup_scalar(g):
-            dst, src = regroup_views(g, 0, GTOK - G_COLS)
-            nc.scalar.copy(out=dst, in_=src)
-
-        def regroup_gpsimd(g):
-            if G_COLS:
-                dst, src = regroup_views(g, GTOK - G_COLS, GTOK)
-                nc.gpsimd.tensor_scalar(out=dst, in0=src, scalar1=1.0, scalar2=0.0, op0=ALU.mult, op1=ALU.add)
+        def regroup(g):
+            hT = S[("hT", g)]
+            hG = hpool.tile([P, GTOK, PACK], BF16, name="hG", align_bytes=64)
+            nc.scalar.copy(
+                out=hG[:].rearrange("p (c i) t -> p c t i", i=4),
+                in_=hT[:].rearrange("p t (c i) -> p c t i", i=4),
+            )
+            S[("hG", g)] = hG
 
         def quantise(g):
             hG = S[("hG", g)]
@@ -182,73 +170,58 @@ def tile_transformerlayer_pa_t_kernel(
             )
             S[("q", g)] = (codes, scl)
 
-        def project(g, pr):
+        def project(g):
             codes, scl = S[("q", g)]
-            bank = psum.tile([P, GT * E], F32, name="mmb", tag="mm%d" % pr)
-            wc = slice(pr * E, (pr + 1) * E)
-            for j in range(GT):
-                tk = slice(j * P, (j + 1) * P)
-                nc.tensor.matmul_mx(
-                    out=bank[:, j * E : (j + 1) * E],
-                    lhsT=codes[:, tk].bitcast(FP8X4),
-                    lhsT_scale=scl[:, tk],
-                    rhs=wcodes[:, wc].bitcast(FP8X4),
-                    rhs_scale=wscl[:, wc],
-                    start=True,
-                    stop=True,
+            banks = []
+            for pr in range(NPROJ):
+                bank = psum.tile([P, GT * E], F32, name="mmb", tag="mm%d" % pr)
+                wc = slice(pr * E, (pr + 1) * E)
+                for j in range(GT):
+                    tk = slice(j * P, (j + 1) * P)
+                    nc.tensor.matmul_mx(
+                        out=bank[:, j * E : (j + 1) * E],
+                        lhsT=codes[:, tk].bitcast(FP8X4),
+                        lhsT_scale=scl[:, tk],
+                        rhs=wcodes[:, wc].bitcast(FP8X4),
+                        rhs_scale=wscl[:, wc],
+                        start=True,
+                        stop=True,
+                    )
+                banks.append(bank)
+            S[("mm", g)] = banks
+
+        def finish(g):
+            banks = S[("mm", g)]
+            o = opool.tile([P, NPROJ, GT * E], F32, name="o")
+            for pr in range(NPROJ):
+                nc.vector.tensor_tensor(
+                    out=o[:, pr, :].rearrange("p (j e) -> p j e", e=E),
+                    in0=banks[pr][:].rearrange("p (j e) -> p j e", e=E),
+                    in1=bias[:, pr, :].unsqueeze(1).to_broadcast([P, GT, E]),
+                    op=ALU.add,
                 )
-            S[("mm", g, pr)] = bank
+                nc.sync.dma_start(out=outs[pr][g], in_=o[:, pr, :])
 
-        def finish(g, pr):
-            if pr == 0:
-                S[("o", g)] = opool.tile([P, NPROJ, GT * E], F32, name="o")
-            o = S[("o", g)]
-            nc.vector.tensor_tensor(
-                out=o[:, pr, :].rearrange("p (j e) -> p j e", e=E),
-                in0=S[("mm", g, pr)][:].rearrange("p (j e) -> p j e", e=E),
-                in1=bias[:, pr, :].unsqueeze(1).to_broadcast([P, GT, E]),
-                op=ALU.add,
-            )
-            nc.sync.dma_start(out=outs[pr][g], in_=o[:, pr, :])
-
-        def drain(u):
-            g, k = divmod(u, UNITS)
-            if k == 0:
-                if g < NG:
-                    quantise(g)
-            else:
-                if g >= 1:
-                    finish(g - 1, k - 1)
-                if g < NG:
-                    project(g, k - 1)
-
-        drained = 0
-        for i in range(-LEAD_STATS, NG + 2):
-            if 0 <= i < NG:
-                affine(i)
-            n = i + LEAD_NORM
-            if 0 <= n < NG:
-                roots(n)
-            if 0 <= i + 1 < NG:
-                transposes(i + 1)
-            if 0 <= i < NG:
-                regroup_scalar(i)
-            for j in range(GT):
-                if 0 <= n < NG:
-                    normalise(n, j)
-                if j == GT - 2 and 0 <= i < NG:
-                    regroup_gpsimd(i)
-            quota = QUOTA_BESIDE_STATS if i + LEAD_STATS < NG else QUOTA_ALONE
-            upto = max(drained, min(UNITS * i, drained + quota))
-            for u in range(drained, upto):
-                drain(u)
-            drained = upto
-            s = i + LEAD_STATS
-            if s < NG:
-                stats(s)
-            if s == 0:
-                gain_rows_to_psum()
-            if s == 1:
-                gain_columns()
-            if s == 2:
-                quantise_weights()
+        ps_setup = None
+        for i in range(NG + 5):
+            if 0 <= i - 1 < NG:
+                rstd_of(i - 1)
+                normalise(i - 1)
+            if 0 <= i - 2 < NG:
+                affine(i - 2)
+            if 0 <= i - 1 < NG:
+                transposes(i - 1)
+            if 0 <= i - 2 < NG:
+                regroup(i - 2)
+            if i < NG:
+                stats(i)
+            if i == 0:
+                ps_setup = setup_a()
+            if i == 1:
+                setup_b(ps_setup)
+            if 0 <= i - 3 < NG:
+                quantise(i - 3)
+            if 0 <= i - 4 < NG:
+                finish(i - 4)
+            if 0 <= i - 3 < NG:
+                project(i - 3)

from contextlib import ExitStack

import concourse.mybir as mybir
from concourse.masks import make_identity

F32 = mybir.dt.float32
BF16 = mybir.dt.bfloat16
U32 = mybir.dt.uint32
U8 = mybir.dt.uint8
FP8X4 = mybir.dt.float8_e4m3fn_x4
ALU = mybir.AluOpType
ACT = mybir.ActivationFunctionType

P = 128
D = 512
PACK = 4
E = 128
NPROJ = 3
TOKENS = 4 * 2048
GT = 4
GTOK = GT * P
NG = TOKENS // GTOK
EPS = 1e-05
TRB = 5

FLOPS = 2 * TOKENS * D * NPROJ * E


def tile_transformerlayer_pa_t_kernel(
    tc, x, ln1_s, ln1_b, wq_k, wq_b, wk_k, wk_b, wv_k, wv_b, out_0, out_1, out_2
):
    nc = tc.nc
    xg = x.rearrange("b s d -> (b s) d").rearrange("(g p j) d -> g p (j d)", p=P, j=GT)
    outs = [
        out_0.rearrange("b s h e -> (b s h) e").rearrange("(g p j) e -> g p (j e)", p=P, j=GT),
        out_1.rearrange("b s e -> (b s) e").rearrange("(g p j) e -> g p (j e)", p=P, j=GT),
        out_2.rearrange("b s e -> (b s) e").rearrange("(g p j) e -> g p (j e)", p=P, j=GT),
    ]

    with ExitStack() as ctx:
        const = ctx.enter_context(tc.tile_pool(name="const", bufs=1))
        xpool = ctx.enter_context(tc.tile_pool(name="xpool", bufs=NG))
        small = ctx.enter_context(tc.tile_pool(name="small", bufs=4))
        zpool = ctx.enter_context(tc.tile_pool(name="zpool", bufs=3))
        hpool = ctx.enter_context(tc.tile_pool(name="hpool", bufs=3))
        qpool = ctx.enter_context(tc.tile_pool(name="qpool", bufs=3))
        opool = ctx.enter_context(tc.tile_pool(name="opool", bufs=4))
        psum = ctx.enter_context(tc.psum_pool(name="psum", bufs=1))

        xt = []
        for g in range(NG):
            x_t = xpool.tile([P, GT, D], BF16, name="x_t")
            nc.sync.dma_start(out=x_t[:].rearrange("p j d -> p (j d)"), in_=xg[g])
            xt.append(x_t)

        sbrow = const.tile([P, P], BF16, name="sbrow")
        nc.vector.memset(sbrow[:], 0.0)
        eps_t = const.tile([P, 1], F32, name="eps_t")
        nc.vector.memset(eps_t[:], EPS)
        nc.scalar.dma_start(out=sbrow[0:PACK, :], in_=ln1_s.rearrange("(t p) -> t p", p=P))
        nc.scalar.dma_start(out=sbrow[PACK : 2 * PACK, :], in_=ln1_b.rearrange("(t p) -> t p", p=P))
        wraw = const.tile([P, PACK, NPROJ * E], BF16, name="wraw")
        nc.scalar.dma_start(out=wraw[:, :, 0:E], in_=wq_k.rearrange("(t p) h e -> p t (h e)", p=P))
        nc.scalar.dma_start(out=wraw[:, :, E : 2 * E], in_=wk_k.rearrange("(t p) e -> p t e", p=P))
        nc.scalar.dma_start(out=wraw[:, :, 2 * E : 3 * E], in_=wv_k.rearrange("(t p) e -> p t e", p=P))

        ident = const.tile([P, P], F32, name="ident")
        make_identity(nc, ident[:])
        bias = const.tile([P, NPROJ, E], BF16, name="bias")
        nc.gpsimd.dma_start(out=bias[:, 0, :], in_=wq_b.rearrange("h e -> (h e)").partition_broadcast(P))
        nc.gpsimd.dma_start(out=bias[:, 1, :], in_=wk_b.partition_broadcast(P))
        nc.gpsimd.dma_start(out=bias[:, 2, :], in_=wv_b.partition_broadcast(P))

        sbcol = const.tile([P, 2 * PACK], F32, name="sbcol")
        wcodes = const.tile([P, NPROJ * E], U32, name="wcodes", align_bytes=64)
        wscl = const.tile([P, NPROJ * E], U8, name="wscl", align_bytes=64)

        def setup_a():
            sbrow32 = const.tile([P, P], F32, name="sbrow32")
            nc.vector.tensor_copy(out=sbrow32[:], in_=sbrow[:])
            ps = psum.tile([P, D], F32, name="ps_setup", tag="mm0")
            nc.tensor.transpose(ps[:, 0:P], sbrow32[:], ident[:])
            return ps

        def setup_b(ps):
            nc.vector.tensor_copy(out=sbcol[:], in_=ps[:, 0 : 2 * PACK])
            wgrp = const.tile([P, NPROJ * E, PACK], BF16, name="wgrp", align_bytes=64)
            nc.vector.tensor_copy(out=wgrp[:], in_=wraw[:].rearrange("p t n -> p n t"))
            for pr in range(NPROJ):
                cols = slice(pr * E, (pr + 1) * E)
                nc.vector.quantize_mx(
                    out=wcodes[:, cols].bitcast(FP8X4),
                    scales=wscl[:, cols],
                    in_=wgrp[:, cols, :].rearrange("p n t -> p (n t)"),
                )

        S = {}

        def stats(g):
            st = small.tile([P, GT, 6], F32, name="st")
            mv = small.tile([P, GT, 2], F32, name="mv")
            for j in range(GT):
                nc.vector.bn_stats(out=st[:, j, :], in_=xt[g][:, j, :])
            for j in range(GT):
                nc.vector.bn_aggr(out=mv[:, j, :], in_=st[:, j, :])
            S[("mv", g)] = mv

        def rstd_of(g):
            mv = S[("mv", g)]
            sd = small.tile([P, GT], F32, name="sd")
            nc.scalar.activation(out=sd[:], in_=mv[:, :, 1], func=ACT.Sqrt, bias=eps_t[:, 0:1], scale=1.0)
            rstd = small.tile([P, GT], F32, name="rstd")
            nc.vector.reciprocal(out=rstd[:], in_=sd[:])
            negmu = small.tile([P, GT], F32, name="negmu")
            nc.vector.tensor_scalar_mul(out=negmu[:], in0=mv[:, :, 0], scalar1=-1.0)
            S[("rs", g)] = (rstd, negmu)

        def normalise(g):
            rstd, negmu = S[("rs", g)]
            z = zpool.tile([P, GT, D], F32, name="z")
            for j in range(GT):
                nc.gpsimd.tensor_scalar(
                    out=z[:, j, :],
                    in0=xt[g][:, j, :],
                    scalar1=negmu[:, j : j + 1],
                    scalar2=rstd[:, j : j + 1],
                    op0=ALU.add,
                    op1=ALU.mult,
                )
            S[("z", g)] = z

        def transposes(g):
            z = S[("z", g)]
            banks = []
            for t in range(PACK):
                bank = psum.tile([P, GTOK], F32, name="trb", tag="tr%d" % ((PACK * g + t) % TRB))
                for j in range(GT):
                    nc.tensor.transpose(bank[:, j * P : (j + 1) * P], z[:, j, t * P : (t + 1) * P], ident[:])
                banks.append(bank)
            S[("tr", g)] = banks

        def affine(g):
            banks = S[("tr", g)]
            hT = hpool.tile([P, PACK, GTOK], BF16, name="hT")
            for t in range(PACK):
                nc.scalar.activation(
                    out=hT[:, t, :],
                    in_=banks[t][:],
                    func=ACT.Identity,
                    scale=sbcol[:, t : t + 1],
                    bias=sbcol[:, PACK + t : PACK + t + 1],
                )
            S[("hT", g)] = hT

        def regroup(g):
            hT = S[("hT", g)]
            hG = hpool.tile([P, GTOK, PACK], BF16, name="hG", align_bytes=64)
            nc.scalar.copy(
                out=hG[:].rearrange("p (c i) t -> p c t i", i=4),
                in_=hT[:].rearrange("p t (c i) -> p c t i", i=4),
            )
            S[("hG", g)] = hG

        def quantise(g):
            hG = S[("hG", g)]
            codes = qpool.tile([P, GTOK], U32, name="codes", align_bytes=64)
            scl = qpool.tile([P, GTOK], U8, name="scl", align_bytes=64)
            nc.vector.quantize_mx(
                out=codes[:].bitcast(FP8X4), scales=scl[:], in_=hG[:].rearrange("p c t -> p (c t)")
            )
            S[("q", g)] = (codes, scl)

        def project(g):
            codes, scl = S[("q", g)]
            banks = []
            for pr in range(NPROJ):
                bank = psum.tile([P, GT * E], F32, name="mmb", tag="mm%d" % pr)
                wc = slice(pr * E, (pr + 1) * E)
                for j in range(GT):
                    tk = slice(j * P, (j + 1) * P)
                    nc.tensor.matmul_mx(
                        out=bank[:, j * E : (j + 1) * E],
                        lhsT=codes[:, tk].bitcast(FP8X4),
                        lhsT_scale=scl[:, tk],
                        rhs=wcodes[:, wc].bitcast(FP8X4),
                        rhs_scale=wscl[:, wc],
                        start=True,
                        stop=True,
                    )
                banks.append(bank)
            S[("mm", g)] = banks

        def finish(g):
            banks = S[("mm", g)]
            o = opool.tile([P, NPROJ, GT * E], F32, name="o")
            for pr in range(NPROJ):
                nc.vector.tensor_tensor(
                    out=o[:, pr, :].rearrange("p (j e) -> p j e", e=E),
                    in0=banks[pr][:].rearrange("p (j e) -> p j e", e=E),
                    in1=bias[:, pr, :].unsqueeze(1).to_broadcast([P, GT, E]),
                    op=ALU.add,
                )
                nc.sync.dma_start(out=outs[pr][g], in_=o[:, pr, :])

        ps_setup = None
        for i in range(NG + 5):
            if 0 <= i - 1 < NG:
                rstd_of(i - 1)
                normalise(i - 1)
            if 0 <= i - 2 < NG:
                affine(i - 2)
            if 0 <= i - 1 < NG:
                transposes(i - 1)
            if 0 <= i - 2 < NG:
                regroup(i - 2)
            if i < NG:
                stats(i)
            if i == 0:
                ps_setup = setup_a()
            if i == 1:
                setup_b(ps_setup)
            if 0 <= i - 3 < NG:
                quantise(i - 3)
            if 0 <= i - 4 < NG:
                finish(i - 4)
            if 0 <= i - 3 < NG:
                project(i - 3)
